import numpy as np
import ml_dtypes


def mxq(x, axis, fmt="e4m3"):
    dtype, down = {"e4m3": (ml_dtypes.float8_e4m3fn, 7), "e5m2": (ml_dtypes.float8_e5m2, 14)}[fmt]
    v = np.moveaxis(np.asarray(x, np.float32).astype(ml_dtypes.bfloat16).astype(np.float64), axis, -1)
    blocks = v.reshape(v.shape[:-1] + (-1, 32))
    amax = np.abs(blocks).max(-1, keepdims=True)
    byte = np.maximum(np.where(amax > 0, np.frexp(amax)[1] - 1 + 127, 0) - down, 1)
    scale = np.exp2(byte - 127.0)
    codes = (blocks / scale).astype(np.float32).astype(dtype).astype(np.float64)
    return np.moveaxis((codes * scale).reshape(v.shape), -1, axis)


WIDE = False


def mx_kscale(k):
    if not WIDE:
        return np.ones(k)
    levels = np.array([10, -10, 5, -5, 0])
    if k % 512:
        return np.exp2(np.random.permutation(np.resize(levels, k // 32))).repeat(32)
    a = np.empty((k // 512, 16))
    for p in range(k // 512):
        a[p, :8] = np.random.permutation(np.resize(levels, 8))
        for g in range(8):
            far = levels[np.abs(levels - a[p, g]) >= 10]
            a[p, g + 8] = far[np.random.randint(len(far))]
    return np.exp2(a.ravel()).repeat(32)


BF16 = ml_dtypes.bfloat16


def bf(x):
    return np.asarray(x, np.float32).astype(BF16)


def f64(x):
    return np.asarray(x).astype(np.float64)


E2M1 = np.array([0.0, 0.5, 1.0, 1.5, 2.0, 3.0, 4.0, 6.0, -0.0, -0.5, -1.0, -1.5, -2.0, -3.0, -4.0, -6.0])


def pack_weight(w, fmt):
    k, n = w.shape
    w = f64(bf(w)).reshape(k // 32, 32, n)
    amax = np.abs(w).max(1)
    if fmt == "e4m3":
        byte = np.frexp(amax)[1] - 1 + 127 - 7
    else:
        mant, ex = np.frexp(amax / 6.0)
        byte = np.where(mant > 0.5, ex, ex - 1) + 127
    byte = np.clip(np.where(amax > 0, byte, 1), 1, 254)
    scaled = (w * np.exp2(127.0 - byte)[:, None, :]).reshape(k, n).astype(np.float32)
    by_word = np.ascontiguousarray(scaled.reshape(k // 512, 128, 4, n).transpose(0, 1, 3, 2))
    if fmt == "e4m3":
        words = by_word.astype(ml_dtypes.float8_e4m3fn).view(np.uint8)
    else:
        c = by_word.astype(ml_dtypes.float4_e2m1fn).view(np.uint8) & 0xF
        words = c[..., 0::2] | (c[..., 1::2] << 4)
    return np.ascontiguousarray(words), np.ascontiguousarray(byte.astype(np.uint8).reshape(k // 512, 16, n))


def unpack_weight(words, scales, fmt):
    g, p, n, _ = words.shape
    if fmt == "e4m3":
        vals = np.ascontiguousarray(words).view(ml_dtypes.float8_e4m3fn).astype(np.float64)
    else:
        nib = np.empty((g, p, n, 4), np.uint8)
        nib[..., 0::2] = words & 0xF
        nib[..., 1::2] = words >> 4
        vals = E2M1[nib]
    vals = vals * np.repeat(np.exp2(scales.astype(np.float64) - 127.0), 8, axis=1)[..., None]
    return vals.transpose(0, 1, 3, 2).reshape(g * 512, n)
def pack4(w):
    words, scales = pack_weight(w, "e2m1")
    return words.reshape(words.shape[0], 128, -1), scales


def unpack4(words, scales):
    return unpack_weight(words.reshape(words.shape[0], 128, -1, 2), scales, "e2m1")


B, N, E, H, NOPE, VDIM, ROPE, QR, KVR = 4, 1024, 1024, 4, 64, 128, 32, 512, 512
QH = NOPE + ROPE
BASE = 10000.0


def rope(v):
    d = v.shape[-1]
    n = v.shape[-2]
    theta = BASE ** (-2.0 * np.arange(d // 2) / d)
    ang = np.arange(n)[:, None] * theta[None, :]
    cos, sin = np.cos(ang), np.sin(ang)
    v1, v2 = v[..., 0::2], v[..., 1::2]
    return np.stack([v1 * cos - v2 * sin, v1 * sin + v2 * cos], axis=-1).reshape(v.shape)


def draw0():
    s, t = mx_kscale(E), mx_kscale(QR)
    x = bf(np.random.standard_normal((B, N, E)) * s)
    Wqa_words, Wqa_scales = pack4(np.random.standard_normal((E, QR)) / np.sqrt(E) / s[:, None] * t)
    Wqb_words, Wqb_scales = pack4(np.random.standard_normal((QR, H * QH)) / np.sqrt(QR) / t[:, None])
    return {"x": x,
            "Wqa_words": Wqa_words, "Wqa_scales": Wqa_scales,
            "Wqb_words": Wqb_words, "Wqb_scales": Wqb_scales}


def core(x, Wqa_words, Wqa_scales, Wqb_words, Wqb_scales):
    cq = mxq(f64(x), 2, "e4m3") @ unpack4(Wqa_words, Wqa_scales)
    q = mxq(cq, 2, "e4m3") @ unpack4(Wqb_words, Wqb_scales)
    q = q.reshape(B, N, H, QH).transpose(0, 2, 1, 3)
    return np.concatenate([q[..., :NOPE], rope(q[..., NOPE:])], axis=-1)


def e4m3fn_bytes(y):
    return np.clip(np.asarray(y, np.float64), -448.0, 448.0).astype(np.float32).astype(ml_dtypes.float8_e4m3fn).view(np.uint8)


def e4m3fn_values(b):
    return np.asarray(b, np.uint8).view(ml_dtypes.float8_e4m3fn).astype(np.float64)


def setup_inputs():
    d = draw0()
    x0 = np.asarray(d['x']).astype(np.float64)
    s = (np.max(np.abs(x0), axis=(0, 1), keepdims=True) / 448.0).astype(np.float32)
    out = {}
    for k, v in d.items():
        if k == 'x':
            out['x_bytes'] = e4m3fn_bytes(x0 / s.astype(np.float64))
            out['x_scale'] = s
        else:
            out[k] = v
    return out


def reference(x_bytes, x_scale, Wqa_words, Wqa_scales, Wqb_words, Wqb_scales):
    return core(e4m3fn_values(x_bytes) * x_scale.astype(np.float64), Wqa_words, Wqa_scales, Wqb_words, Wqb_scales)

@@ -1,0 +1,298 @@
+import math
+from contextlib import ExitStack
+
+import concourse.mybir as mybir
+from concourse.masks import make_identity
+
+F32 = mybir.dt.float32
+BF16 = mybir.dt.bfloat16
+I32 = mybir.dt.int32
+U32 = mybir.dt.uint32
+U8 = mybir.dt.uint8
+FP8 = mybir.dt.float8_e4m3fn
+FP8X4 = mybir.dt.float8_e4m3fn_x4
+FP4X4 = mybir.dt.float4_e2m1fn_x4
+ALU = mybir.AluOpType
+ACT = mybir.ActivationFunctionType
+
+B, N, E, H, NOPE, ROPE, QR = 4, 1024, 1024, 4, 64, 32, 512
+QH = NOPE + ROPE
+PAIRS = ROPE // 2
+P = 128
+G1 = E // 512
+TOK = 4
+GROUPS = B * N // (P * TOK)
+HALVES = N // (P * TOK)
+STEPS = GROUPS * 2
+TWO_PI = 2.0 * math.pi
+
+FLOPS = 2 * B * N * (E * QR + QR * H * QH)
+
+
+def tile_multilatentattention_pa_t_w4_kernel(
+    tc, x_bytes, x_scale, Wqa_words, Wqa_scales, Wqb_words, Wqb_scales, out
+):
+    nc = tc.nc
+    with ExitStack() as ctx:
+        keep = ctx.enter_context(tc.tile_pool(name="keep", bufs=1))
+        xin = ctx.enter_context(tc.tile_pool(name="xin", bufs=GROUPS))
+        work = ctx.enter_context(tc.tile_pool(name="work", bufs=4))
+        outp = ctx.enter_context(tc.tile_pool(name="outp", bufs=3))
+        psum = ctx.enter_context(tc.psum_pool(name="psum", bufs=2))
+        ctx.enter_context(tc.manual_schedule())
+
+        npos = HALVES * TOK
+        pos = keep.tile([P, npos], F32, align_bytes=64)
+        nc.gpsimd.iota(
+            pos[:], pattern=[[P * TOK, HALVES], [1, TOK]], base=0, channel_multiplier=TOK,
+            allow_small_or_imprecise_dtypes=True,
+        )
+        scale_row = keep.tile([P, E], F32, align_bytes=64)
+        wqa_raw = keep.tile([P, G1, 2 * QR], U8, align_bytes=64)
+        wqa_raw_s = keep.tile([P, G1, QR], U8, align_bytes=64)
+        wqb = keep.tile([P, 2 * H * QH], U8, align_bytes=64)
+        wqb_s = keep.tile([P, H * QH], U8, align_bytes=64)
+        nc.gpsimd.memset(wqa_raw_s[:].rearrange("p g n -> p (g n)").bitcast(I32), 0)
+        nc.gpsimd.memset(wqb_s[:].bitcast(I32), 0)
+
+        x_view = x_bytes.rearrange("b (f p j) k -> (b f) p j k", f=HALVES, p=P, j=TOK)
+        x_tiles = []
+        for g in range(GROUPS):
+            xb = xin.tile([P, TOK, E], U8, align_bytes=64)
+            x_tiles.append(xb)
+        nc.scalar.dma_start(
+            out=scale_row[:], in_=x_scale.rearrange("a b k -> (a b k)").partition_broadcast(P)
+        )
+        nc.sync.dma_start(out=wqa_raw[:], in_=Wqa_words.rearrange("g p n -> p g n"))
+        sa = Wqa_scales.rearrange("g (q r) n -> r q g n", r=4)
+        for r in range(4):
+            nc.sync.dma_start(
+                out=wqa_raw_s[r:P:32].bitcast(I32), in_=sa[r].bitcast(I32)
+            )
+        for j in range(TOK):
+            nc.sync.dma_start(out=x_tiles[0][:, j, :], in_=x_view[0][:, j, :])
+        nc.sync.dma_start(out=x_tiles[1][:], in_=x_view[1])
+        nb = H * NOPE
+        wb = Wqb_words.rearrange("g p (h c) -> (g p) h c", h=H)
+        nc.sync.dma_start(
+            out=wqb[:, 0 : 2 * nb].rearrange("p (h c) -> p h c", h=H), in_=wb[:, :, 0 : 2 * NOPE]
+        )
+        nc.sync.dma_start(
+            out=wqb[:, 2 * nb :].rearrange("p (h c) -> p h c", h=H), in_=wb[:, :, 2 * NOPE :]
+        )
+        sb = Wqb_scales.rearrange("g (q r) (h c) -> r (g q) h c", r=4, h=H)
+        for r in range(4):
+            nc.sync.dma_start(
+                out=wqb_s[r:P:32, 0:nb].rearrange("q (h c) -> q h c", h=H).bitcast(I32),
+                in_=sb[r][:, :, 0:NOPE].bitcast(I32),
+            )
+            nc.sync.dma_start(
+                out=wqb_s[r:P:32, nb:].rearrange("q (h c) -> q h c", h=H).bitcast(I32),
+                in_=sb[r][:, :, NOPE:].bitcast(I32),
+            )
+        for g in range(2, GROUPS):
+            nc.sync.dma_start(out=x_tiles[g][:], in_=x_view[g])
+
+        ident = keep.tile([P, P], F32, align_bytes=64)
+        make_identity(nc, ident[:])
+        turns = keep.tile([P, 2, npos, PAIRS], F32, align_bytes=64)
+        whole = keep.tile([P, 2, npos, PAIRS], I32, align_bytes=64)
+        frac = keep.tile([P, 2, npos, PAIRS], F32, align_bytes=64)
+        over = keep.tile([P, 2, npos, PAIRS], F32, align_bytes=64)
+        cos_t = keep.tile([P, HALVES, TOK, ROPE], F32, align_bytes=64)
+        sin_t = keep.tile([P, HALVES, TOK, ROPE], F32, align_bytes=64)
+
+        def tables():
+            for i in range(PAIRS):
+                per_pos = 10000.0 ** (-2.0 * i / ROPE) / TWO_PI
+                nc.vector.tensor_scalar(turns[:, 0, :, i], pos[:], per_pos, None, op0=ALU.mult)
+            nc.vector.tensor_scalar(turns[:, 1], turns[:, 0], 0.25, None, op0=ALU.add)
+            nc.vector.tensor_copy(out=whole[:], in_=turns[:])
+            nc.vector.tensor_tensor(out=frac[:], in0=turns[:], in1=whole[:], op=ALU.subtract)
+            nc.vector.scalar_tensor_tensor(
+                out=over[:], in0=frac[:], scalar=0.5, in1=frac[:], op0=ALU.is_gt, op1=ALU.subtract
+            )
+            c = cos_t[:].rearrange("p f j (i e) -> p (f j) i e", e=2)
+            s = sin_t[:].rearrange("p f j (i e) -> p (f j) i e", e=2)
+            for e in range(2):
+                nc.scalar.activation(c[:, :, :, e], over[:, 1], ACT.Sin, scale=-TWO_PI)
+                nc.scalar.activation(s[:, :, :, e], over[:, 0], ACT.Sin, scale=(TWO_PI, -TWO_PI)[e])
+
+        wqa = keep.tile([P, G1, 2 * QR], U8, align_bytes=64)
+        wqa_s = keep.tile([P, G1, QR], U8, align_bytes=64)
+
+        def permute_words():
+            for g in range(G1):
+                nc.vector.tensor_copy(
+                    out=wqa[:, g].rearrange("p (j m b) -> p j m b", j=4, b=2),
+                    in_=wqa_raw[:, g].rearrange("p (m j b) -> p j m b", j=4, b=2),
+                )
+
+        def permute_scales():
+            for g in range(G1):
+                nc.vector.tensor_copy(
+                    out=wqa_s[:, g].rearrange("p (j m) -> p j m", j=4),
+                    in_=wqa_raw_s[:, g].rearrange("p (m j) -> p j m", j=4),
+                )
+
+        xbf, xg, xq, xs = {}, {}, {}, {}
+        cqb, cg, cq, cs = {}, {}, {}, {}
+        nopes, ropes, ots = {}, {}, {}
+        xts = {}
+
+        def widen(s):
+            t = work.tile([P, 2, E], BF16, align_bytes=64, name="xbf")
+            xbf[s] = t
+            for i in range(2):
+                nc.vector.tensor_tensor(
+                    out=t[:, i, :],
+                    in0=x_tiles[s // 2][:, 2 * (s % 2) + i, :].bitcast(FP8),
+                    in1=scale_row[:],
+                    op=ALU.mult,
+                )
+
+        def turn(s):
+            words = xbf[s][:].rearrange("p j k -> p (j k)").bitcast(F32)
+            for i in range(2):
+                xt = psum.tile([P, G1, 2, P], F32, name="xt")
+                xts[s, i] = xt
+                for g in range(G1):
+                    for u in range(2):
+                        lo = 512 * i + 256 * g
+                        nc.tensor.transpose(xt[:, g, u, :], words[:, lo + u : lo + 256 : 2], ident[:])
+
+        def take_x(s):
+            t = work.tile([P, 2, G1, P, 4], BF16, align_bytes=64, name="xg")
+            xg[s] = t
+            for i in range(2):
+                nc.scalar.copy(
+                    out=t[:, i].rearrange("p g r t -> p (g r t)").bitcast(F32),
+                    in_=xts[s, i][:].rearrange("p g u r -> p g r u"),
+                )
+
+        def quant_x(s):
+            q = work.tile([P, 2, G1, P], U32, align_bytes=64, name="xq")
+            sc = work.tile([P, 2, G1, P], U8, align_bytes=64, name="xs")
+            xq[s], xs[s] = q, sc
+            nc.vector.quantize_mx(
+                out=q[:].rearrange("p i g r -> p (i g r)").bitcast(FP8X4),
+                scales=sc[:].rearrange("p i g r -> p (i g r)"),
+                in_=xg[s][:].rearrange("p i g r t -> p (i g r t)"),
+            )
+
+        def first(s):
+            for i in range(2):
+                acc = psum.tile([P, 4, P], F32, name="cqp")
+                cqb[s, i] = acc
+                for j in range(4):
+                    for g in range(G1):
+                        nc.tensor.matmul_mx(
+                            out=acc[:, j, :],
+                            lhsT=wqa[:, g, 2 * P * j : 2 * P * (j + 1)].bitcast(FP4X4),
+                            lhsT_scale=wqa_s[:, g, P * j : P * (j + 1)],
+                            rhs=xq[s][:, i, g, :].bitcast(FP8X4),
+                            rhs_scale=xs[s][:, i, g, :],
+                            start=(g == 0),
+                            stop=(g == G1 - 1),
+                        )
+
+        def take_cq(s):
+            t = work.tile([P, 2, P, 4], BF16, align_bytes=64, name="cg")
+            cg[s] = t
+            for i in range(2):
+                nc.scalar.copy(out=t[:, i], in_=cqb[s, i][:].rearrange("p j r -> p r j"))
+
+        def quant_cq(s):
+            q = work.tile([P, 2, P], U32, align_bytes=64, name="cq")
+            sc = work.tile([P, 2, P], U8, align_bytes=64, name="cs")
+            cq[s], cs[s] = q, sc
+            nc.vector.quantize_mx(
+                out=q[:].rearrange("p i r -> p (i r)").bitcast(FP8X4),
+                scales=sc[:].rearrange("p i r -> p (i r)"),
+                in_=cg[s][:].rearrange("p i r t -> p (i r t)"),
+            )
+
+        def second(s):
+            if s % 2 == 0:
+                rp = psum.tile([P, TOK, H * ROPE], F32, name="rope")
+                ropes[s // 2] = rp
+            npe = psum.tile([P, 2, nb], F32, name="nope")
+            nopes[s] = npe
+            rp = ropes[s // 2]
+            for i in range(2):
+                for dst, lo, hi in ((npe[:, i, :], 0, nb), (rp[:, 2 * (s % 2) + i, :], nb, H * QH)):
+                    nc.tensor.matmul_mx(
+                        out=dst,
+                        lhsT=cq[s][:, i, :].bitcast(FP8X4),
+                        lhsT_scale=cs[s][:, i, :],
+                        rhs=wqb[:, 2 * lo : 2 * hi].bitcast(FP4X4),
+                        rhs_scale=wqb_s[:, lo:hi],
+                        start=True,
+                        stop=True,
+                    )
+
+        def take_nope(s):
+            if s % 2 == 0:
+                o = outp.tile([P, H, TOK, QH], F32, align_bytes=64, name="o")
+                ots[s // 2] = o
+            j0 = 2 * (s % 2)
+            nc.scalar.copy(
+                out=ots[s // 2][:, :, j0 : j0 + 2, 0:NOPE].rearrange("p h j c -> p j h c"),
+                in_=nopes[s][:].rearrange("p j (h c) -> p j h c", h=H),
+            )
+
+        def rope(grp, j0, nj):
+            src = ropes[grp][:, j0 : j0 + nj, :].rearrange("p j (h i e) -> p j h i e", h=H, e=2)
+            f = grp % HALVES
+            cosv = cos_t[:, f, j0 : j0 + nj, :].unsqueeze(2).to_broadcast([P, nj, H, ROPE])
+            sinv = sin_t[:, f, j0 : j0 + nj, :].unsqueeze(2).to_broadcast([P, nj, H, ROPE])
+            ra = work.tile([P, TOK, H, ROPE], F32, align_bytes=64, name="ra")
+            rb = work.tile([P, TOK, H, ROPE], F32, align_bytes=64, name="rb")
+            nc.vector.tensor_tensor(
+                out=ra[:, 0:nj], in0=src.rearrange("p j h i e -> p j h (i e)"), in1=cosv, op=ALU.mult
+            )
+            nc.vector.tensor_tensor(
+                out=rb[:, 0:nj].rearrange("p j h (i e) -> p j h i e", e=2),
+                in0=src[:, :, :, :, ::-1],
+                in1=sinv.rearrange("p j h (i e) -> p j h i e", e=2),
+                op=ALU.mult,
+            )
+            nc.vector.tensor_tensor(
+                out=ots[grp][:, :, j0 : j0 + nj, NOPE:].rearrange("p h j c -> p j h c"),
+                in0=ra[:, 0:nj],
+                in1=rb[:, 0:nj],
+                op=ALU.add,
+            )
+
+        def store(grp, j0, nj):
+            dst = out[grp // HALVES].rearrange("h (f p j) c -> f p h j c", f=HALVES, j=TOK)[grp % HALVES]
+            nc.sync.dma_start(out=dst[:, :, j0 : j0 + nj, :], in_=ots[grp][:, :, j0 : j0 + nj, :])
+
+        tables()
+        permute_words()
+        widen(0)
+        permute_scales()
+        for s in range(STEPS + 3):
+            if s + 1 < STEPS:
+                widen(s + 1)
+            if s < STEPS:
+                turn(s)
+                take_x(s)
+                quant_x(s)
+            if s >= 3:
+                second(s - 3)
+                take_nope(s - 3)
+            if 1 <= s <= STEPS:
+                first(s - 1)
+                take_cq(s - 1)
+            if s >= 3:
+                k = s - 3
+                grp = k // 2
+                if grp == GROUPS - 1:
+                    rope(grp, 2 * (k % 2), 2)
+                    store(grp, 2 * (k % 2), 2)
+                elif k % 2 == 1:
+                    rope(grp, 0, TOK)
+                    store(grp, 0, TOK)
+            if 1 <= s <= STEPS:
+                quant_cq(s - 1)

@@ -52,6 +52,8 @@ def tile_multilatentattention_pa_t_w4_kernel(
         wqa_raw_s = keep.tile([P, G1, QR], U8, align_bytes=64)
         wqb = keep.tile([P, 2 * H * QH], U8, align_bytes=64)
         wqb_s = keep.tile([P, H * QH], U8, align_bytes=64)
+        ident = keep.tile([P, P], F32, align_bytes=64)
+        make_identity(nc, ident[:])
         nc.gpsimd.memset(wqa_raw_s[:].rearrange("p g n -> p (g n)").bitcast(I32), 0)
         nc.gpsimd.memset(wqb_s[:].bitcast(I32), 0)
 
@@ -60,9 +62,8 @@ def tile_multilatentattention_pa_t_w4_kernel(
         for g in range(GROUPS):
             xb = xin.tile([P, TOK, E], U8, align_bytes=64)
             x_tiles.append(xb)
-        nc.scalar.dma_start(
-            out=scale_row[:], in_=x_scale.rearrange("a b k -> (a b k)").partition_broadcast(P)
-        )
+        sv = keep.tile([P, E // P], F32, align_bytes=64)
+        nc.sync.dma_start(out=sv[:], in_=x_scale.rearrange("a b (n m) -> (a b n) m", n=P))
         nc.sync.dma_start(out=wqa_raw[:], in_=Wqa_words.rearrange("g p n -> p g n"))
         sa = Wqa_scales.rearrange("g (q r) n -> r q g n", r=4)
         for r in range(4):
@@ -93,8 +94,19 @@ def tile_multilatentattention_pa_t_w4_kernel(
         for g in range(2, GROUPS):
             nc.sync.dma_start(out=x_tiles[g][:], in_=x_view[g])
 
-        ident = keep.tile([P, P], F32, align_bytes=64)
-        make_identity(nc, ident[:])
+        def spread_scales():
+            for h in range(2):
+                bank = psum.tile([P, 4, P], F32, name="xt")
+                for m in range(4):
+                    c = 4 * h + m
+                    nc.tensor.transpose(bank[:, m, :], sv[:, c : c + 1].to_broadcast([P, P]), ident[:])
+                dst = scale_row[:].rearrange("p (n h m) -> p h n m", h=2, m=4)[:, h]
+                src = bank[:].rearrange("p m n -> p n m")
+                if h == 0:
+                    nc.scalar.copy(out=dst, in_=src)
+                else:
+                    nc.vector.tensor_copy(out=dst, in_=src)
+
         turns = keep.tile([P, 2, npos, PAIRS], F32, align_bytes=64)
         whole = keep.tile([P, 2, npos, PAIRS], I32, align_bytes=64)
         frac = keep.tile([P, 2, npos, PAIRS], F32, align_bytes=64)
@@ -241,26 +253,39 @@ def tile_multilatentattention_pa_t_w4_kernel(
                 in_=nopes[s][:].rearrange("p j (h c) -> p j h c", h=H),
             )
 
-        def rope(grp, j0, nj):
-            src = ropes[grp][:, j0 : j0 + nj, :].rearrange("p j (h i e) -> p j h i e", h=H, e=2)
-            f = grp % HALVES
-            cosv = cos_t[:, f, j0 : j0 + nj, :].unsqueeze(2).to_broadcast([P, nj, H, ROPE])
-            sinv = sin_t[:, f, j0 : j0 + nj, :].unsqueeze(2).to_broadcast([P, nj, H, ROPE])
-            ra = work.tile([P, TOK, H, ROPE], F32, align_bytes=64, name="ra")
-            rb = work.tile([P, TOK, H, ROPE], F32, align_bytes=64, name="rb")
+        ras, rbs = {}, {}
+
+        def views(grp, j0, j1):
+            src = ropes[grp][:, j0:j1, :].rearrange("p j (h i e) -> p j h i e", h=H, e=2)
+            shape = [P, j1 - j0, H, ROPE]
+            cosv = cos_t[:, grp % HALVES, j0:j1, :].unsqueeze(2).to_broadcast(shape)
+            sinv = sin_t[:, grp % HALVES, j0:j1, :].unsqueeze(2).to_broadcast(shape)
+            return src, cosv, sinv
+
+        def rope_cos(grp, j0, j1):
+            if j0 == 0:
+                ra = work.tile([P, TOK, H, ROPE], F32, align_bytes=64, name="ra")
+                rb = work.tile([P, TOK, H, ROPE], F32, align_bytes=64, name="rb")
+                ras[grp], rbs[grp] = ra, rb
+            src, cosv, sinv = views(grp, j0, j1)
             nc.vector.tensor_tensor(
-                out=ra[:, 0:nj], in0=src.rearrange("p j h i e -> p j h (i e)"), in1=cosv, op=ALU.mult
+                out=ras[grp][:, j0:j1], in0=src.rearrange("p j h i e -> p j h (i e)"), in1=cosv, op=ALU.mult
             )
+
+        def rope_sin(grp, j0, j1):
+            src, cosv, sinv = views(grp, j0, j1)
             nc.vector.tensor_tensor(
-                out=rb[:, 0:nj].rearrange("p j h (i e) -> p j h i e", e=2),
+                out=rbs[grp][:, j0:j1].rearrange("p j h (i e) -> p j h i e", e=2),
                 in0=src[:, :, :, :, ::-1],
                 in1=sinv.rearrange("p j h (i e) -> p j h i e", e=2),
                 op=ALU.mult,
             )
-            nc.vector.tensor_tensor(
-                out=ots[grp][:, :, j0 : j0 + nj, NOPE:].rearrange("p h j c -> p j h c"),
-                in0=ra[:, 0:nj],
-                in1=rb[:, 0:nj],
+
+        def rope_add(eng, grp, j0, j1):
+            eng.tensor_tensor(
+                out=ots[grp][:, :, j0:j1, NOPE:].rearrange("p h j c -> p j h c"),
+                in0=ras[grp][:, j0:j1],
+                in1=rbs[grp][:, j0:j1],
                 op=ALU.add,
             )
 
@@ -270,6 +295,7 @@ def tile_multilatentattention_pa_t_w4_kernel(
 
         tables()
         permute_words()
+        spread_scales()
         widen(0)
         permute_scales()
         for s in range(STEPS + 3):
@@ -288,11 +314,19 @@ def tile_multilatentattention_pa_t_w4_kernel(
             if s >= 3:
                 k = s - 3
                 grp = k // 2
-                if grp == GROUPS - 1:
-                    rope(grp, 2 * (k % 2), 2)
-                    store(grp, 2 * (k % 2), 2)
+                last = grp == GROUPS - 1
+                if grp > 0 and k % 2 == (0 if last else 1):
+                    rope_sin(grp - 1, TOK - 1, TOK)
+                    rope_add(nc.gpsimd, grp - 1, 0, TOK)
+                    store(grp - 1, 0, TOK)
+                if last:
+                    j0 = 2 * (k % 2)
+                    rope_cos(grp, j0, j0 + 2)
+                    rope_sin(grp, j0, j0 + 2)
+                    rope_add(nc.vector, grp, j0, j0 + 2)
+                    store(grp, j0, 2)
                 elif k % 2 == 1:
-                    rope(grp, 0, TOK)
-                    store(grp, 0, TOK)
+                    rope_cos(grp, 0, TOK)
+                    rope_sin(grp, 0, TOK - 1)
             if 1 <= s <= STEPS:
                 quant_cq(s - 1)

@@ -298,21 +298,19 @@ def tile_multilatentattention_pa_t_w4_kernel(
         spread_scales()
         widen(0)
         permute_scales()
-        for s in range(STEPS + 3):
+        for s in range(STEPS + 7):
+            if 0 <= s - 2 < STEPS:
+                quant_x(s - 2)
             if s + 1 < STEPS:
                 widen(s + 1)
+            if 0 <= s - 3 < STEPS:
+                first(s - 3)
+                take_cq(s - 3)
             if s < STEPS:
                 turn(s)
                 take_x(s)
-                quant_x(s)
-            if s >= 3:
-                second(s - 3)
-                take_nope(s - 3)
-            if 1 <= s <= STEPS:
-                first(s - 1)
-                take_cq(s - 1)
-            if s >= 3:
-                k = s - 3
+            k = s - 6
+            if 0 <= k < STEPS:
                 grp = k // 2
                 last = grp == GROUPS - 1
                 if grp > 0 and k % 2 == (0 if last else 1):
@@ -328,5 +326,8 @@ def tile_multilatentattention_pa_t_w4_kernel(
                 elif k % 2 == 1:
                     rope_cos(grp, 0, TOK)
                     rope_sin(grp, 0, TOK - 1)
-            if 1 <= s <= STEPS:
-                quant_cq(s - 1)
+            if 0 <= s - 5 < STEPS:
+                second(s - 5)
+                take_nope(s - 5)
+            if 0 <= s - 4 < STEPS:
+                quant_cq(s - 4)

@@ -37,9 +37,14 @@ def tile_multilatentattention_pa_t_w4_kernel(
         keep = ctx.enter_context(tc.tile_pool(name="keep", bufs=1))
         xin = ctx.enter_context(tc.tile_pool(name="xin", bufs=GROUPS))
         work = ctx.enter_context(tc.tile_pool(name="work", bufs=4))
-        outp = ctx.enter_context(tc.tile_pool(name="outp", bufs=3))
+        outp = ctx.enter_context(tc.tile_pool(name="outp", bufs=5))
         psum = ctx.enter_context(tc.psum_pool(name="psum", bufs=2))
+        psum_n = ctx.enter_context(tc.psum_pool(name="psum_n", bufs=1))
+        psum_r = ctx.enter_context(tc.psum_pool(name="psum_r", bufs=3))
         ctx.enter_context(tc.manual_schedule())
+
+        zeros = keep.tile([P, 512], BF16, align_bytes=64)
+        nc.vector.memset(zeros[:].bitcast(I32), 0)
 
         npos = HALVES * TOK
         pos = keep.tile([P, npos], F32, align_bytes=64)
@@ -47,7 +52,7 @@ def tile_multilatentattention_pa_t_w4_kernel(
             pos[:], pattern=[[P * TOK, HALVES], [1, TOK]], base=0, channel_multiplier=TOK,
             allow_small_or_imprecise_dtypes=True,
         )
-        scale_row = keep.tile([P, E], F32, align_bytes=64)
+        scale_row = keep.tile([P, 2, E], F32, align_bytes=64)
         wqa_raw = keep.tile([P, G1, 2 * QR], U8, align_bytes=64)
         wqa_raw_s = keep.tile([P, G1, QR], U8, align_bytes=64)
         wqb = keep.tile([P, 2 * H * QH], U8, align_bytes=64)
@@ -94,18 +99,24 @@ def tile_multilatentattention_pa_t_w4_kernel(
         for g in range(2, GROUPS):
             nc.sync.dma_start(out=x_tiles[g][:], in_=x_view[g])
 
+        def warm(n):
+            bank = psum.tile([P, 512], F32, name="xt")
+            for i in range(n):
+                nc.tensor.matmul(bank[:], lhsT=zeros[:, 0:P], rhs=zeros[:], start=True, stop=True)
+
         def spread_scales():
             for h in range(2):
                 bank = psum.tile([P, 4, P], F32, name="xt")
                 for m in range(4):
                     c = 4 * h + m
                     nc.tensor.transpose(bank[:, m, :], sv[:, c : c + 1].to_broadcast([P, P]), ident[:])
-                dst = scale_row[:].rearrange("p (n h m) -> p h n m", h=2, m=4)[:, h]
+                dst = scale_row[:, 0, :].rearrange("p (n h m) -> p h n m", h=2, m=4)[:, h]
                 src = bank[:].rearrange("p m n -> p n m")
                 if h == 0:
                     nc.scalar.copy(out=dst, in_=src)
                 else:
                     nc.vector.tensor_copy(out=dst, in_=src)
+            nc.scalar.copy(out=scale_row[:, 1, :], in_=scale_row[:, 0, :])
 
         turns = keep.tile([P, 2, npos, PAIRS], F32, align_bytes=64)
         whole = keep.tile([P, 2, npos, PAIRS], I32, align_bytes=64)
@@ -155,11 +166,13 @@ def tile_multilatentattention_pa_t_w4_kernel(
         def widen(s):
             t = work.tile([P, 2, E], BF16, align_bytes=64, name="xbf")
             xbf[s] = t
-            for i in range(2):
+            j0 = 2 * (s % 2)
+            n = 1 if s == 0 else 2
+            for i in range(0, 2, n):
                 nc.vector.tensor_tensor(
-                    out=t[:, i, :],
-                    in0=x_tiles[s // 2][:, 2 * (s % 2) + i, :].bitcast(FP8),
-                    in1=scale_row[:],
+                    out=t[:, i : i + n, :].rearrange("p j k -> p (j k)"),
+                    in0=x_tiles[s // 2][:, j0 + i : j0 + i + n, :].rearrange("p j k -> p (j k)").bitcast(FP8),
+                    in1=scale_row[:, 0:n, :].rearrange("p j k -> p (j k)"),
                     op=ALU.mult,
                 )
 
@@ -226,9 +239,9 @@ def tile_multilatentattention_pa_t_w4_kernel(
 
         def second(s):
             if s % 2 == 0:
-                rp = psum.tile([P, TOK, H * ROPE], F32, name="rope")
+                rp = psum_r.tile([P, TOK, H * ROPE], F32, name="rope")
                 ropes[s // 2] = rp
-            npe = psum.tile([P, 2, nb], F32, name="nope")
+            npe = psum_n.tile([P, 2, nb], F32, name="nope")
             nopes[s] = npe
             rp = ropes[s // 2]
             for i in range(2):
@@ -293,23 +306,21 @@ def tile_multilatentattention_pa_t_w4_kernel(
             dst = out[grp // HALVES].rearrange("h (f p j) c -> f p h j c", f=HALVES, j=TOK)[grp % HALVES]
             nc.sync.dma_start(out=dst[:, :, j0 : j0 + nj, :], in_=ots[grp][:, :, j0 : j0 + nj, :])
 
+        warm(5)
         tables()
         permute_words()
         spread_scales()
+        warm(3)
         widen(0)
         permute_scales()
-        for s in range(STEPS + 7):
+        for s in range(STEPS + 8):
             if 0 <= s - 2 < STEPS:
                 quant_x(s - 2)
             if s + 1 < STEPS:
                 widen(s + 1)
-            if 0 <= s - 3 < STEPS:
-                first(s - 3)
-                take_cq(s - 3)
-            if s < STEPS:
-                turn(s)
-                take_x(s)
-            k = s - 6
+            if 0 <= s - 4 < STEPS:
+                quant_cq(s - 4)
+            k = s - 7
             if 0 <= k < STEPS:
                 grp = k // 2
                 last = grp == GROUPS - 1
@@ -326,8 +337,12 @@ def tile_multilatentattention_pa_t_w4_kernel(
                 elif k % 2 == 1:
                     rope_cos(grp, 0, TOK)
                     rope_sin(grp, 0, TOK - 1)
+            if 0 <= s - 3 < STEPS:
+                first(s - 3)
+                take_cq(s - 3)
+            if s < STEPS:
+                turn(s)
+                take_x(s)
             if 0 <= s - 5 < STEPS:
                 second(s - 5)
                 take_nope(s - 5)
-            if 0 <= s - 4 < STEPS:
-                quant_cq(s - 4)

import math
from contextlib import ExitStack

import concourse.mybir as mybir
from concourse.masks import make_identity

F32 = mybir.dt.float32
BF16 = mybir.dt.bfloat16
I32 = mybir.dt.int32
U32 = mybir.dt.uint32
U8 = mybir.dt.uint8
FP8 = mybir.dt.float8_e4m3fn
FP8X4 = mybir.dt.float8_e4m3fn_x4
FP4X4 = mybir.dt.float4_e2m1fn_x4
ALU = mybir.AluOpType
ACT = mybir.ActivationFunctionType

B, N, E, H, NOPE, ROPE, QR = 4, 1024, 1024, 4, 64, 32, 512
QH = NOPE + ROPE
PAIRS = ROPE // 2
P = 128
G1 = E // 512
TOK = 4
GROUPS = B * N // (P * TOK)
HALVES = N // (P * TOK)
STEPS = GROUPS * 2
TWO_PI = 2.0 * math.pi

FLOPS = 2 * B * N * (E * QR + QR * H * QH)


def tile_multilatentattention_pa_t_w4_kernel(
    tc, x_bytes, x_scale, Wqa_words, Wqa_scales, Wqb_words, Wqb_scales, out
):
    nc = tc.nc
    with ExitStack() as ctx:
        keep = ctx.enter_context(tc.tile_pool(name="keep", bufs=1))
        xin = ctx.enter_context(tc.tile_pool(name="xin", bufs=GROUPS))
        work = ctx.enter_context(tc.tile_pool(name="work", bufs=4))
        outp = ctx.enter_context(tc.tile_pool(name="outp", bufs=5))
        psum = ctx.enter_context(tc.psum_pool(name="psum", bufs=2))
        psum_n = ctx.enter_context(tc.psum_pool(name="psum_n", bufs=1))
        psum_r = ctx.enter_context(tc.psum_pool(name="psum_r", bufs=3))
        ctx.enter_context(tc.manual_schedule())

        zeros = keep.tile([P, 512], BF16, align_bytes=64)
        nc.vector.memset(zeros[:].bitcast(I32), 0)

        npos = HALVES * TOK
        pos = keep.tile([P, npos], F32, align_bytes=64)
        nc.gpsimd.iota(
            pos[:], pattern=[[P * TOK, HALVES], [1, TOK]], base=0, channel_multiplier=TOK,
            allow_small_or_imprecise_dtypes=True,
        )
        scale_row = keep.tile([P, 2, E], F32, align_bytes=64)
        wqa_raw = keep.tile([P, G1, 2 * QR], U8, align_bytes=64)
        wqa_raw_s = keep.tile([P, G1, QR], U8, align_bytes=64)
        wqb = keep.tile([P, 2 * H * QH], U8, align_bytes=64)
        wqb_s = keep.tile([P, H * QH], U8, align_bytes=64)
        ident = keep.tile([P, P], F32, align_bytes=64)
        make_identity(nc, ident[:])
        nc.gpsimd.memset(wqa_raw_s[:].rearrange("p g n -> p (g n)").bitcast(I32), 0)
        nc.gpsimd.memset(wqb_s[:].bitcast(I32), 0)

        x_view = x_bytes.rearrange("b (f p j) k -> (b f) p j k", f=HALVES, p=P, j=TOK)
        x_tiles = []
        for g in range(GROUPS):
            xb = xin.tile([P, TOK, E], U8, align_bytes=64)
            x_tiles.append(xb)
        sv = keep.tile([P, E // P], F32, align_bytes=64)
        nc.sync.dma_start(out=sv[:], in_=x_scale.rearrange("a b (n m) -> (a b n) m", n=P))
        nc.sync.dma_start(out=wqa_raw[:], in_=Wqa_words.rearrange("g p n -> p g n"))
        sa = Wqa_scales.rearrange("g (q r) n -> r q g n", r=4)
        for r in range(4):
            nc.sync.dma_start(
                out=wqa_raw_s[r:P:32].bitcast(I32), in_=sa[r].bitcast(I32)
            )
        for j in range(TOK):
            nc.sync.dma_start(out=x_tiles[0][:, j, :], in_=x_view[0][:, j, :])
        nc.sync.dma_start(out=x_tiles[1][:], in_=x_view[1])
        nb = H * NOPE
        wb = Wqb_words.rearrange("g p (h c) -> (g p) h c", h=H)
        nc.sync.dma_start(
            out=wqb[:, 0 : 2 * nb].rearrange("p (h c) -> p h c", h=H), in_=wb[:, :, 0 : 2 * NOPE]
        )
        nc.sync.dma_start(
            out=wqb[:, 2 * nb :].rearrange("p (h c) -> p h c", h=H), in_=wb[:, :, 2 * NOPE :]
        )
        sb = Wqb_scales.rearrange("g (q r) (h c) -> r (g q) h c", r=4, h=H)
        for r in range(4):
            nc.sync.dma_start(
                out=wqb_s[r:P:32, 0:nb].rearrange("q (h c) -> q h c", h=H).bitcast(I32),
                in_=sb[r][:, :, 0:NOPE].bitcast(I32),
            )
            nc.sync.dma_start(
                out=wqb_s[r:P:32, nb:].rearrange("q (h c) -> q h c", h=H).bitcast(I32),
                in_=sb[r][:, :, NOPE:].bitcast(I32),
            )
        for g in range(2, GROUPS):
            nc.sync.dma_start(out=x_tiles[g][:], in_=x_view[g])

        def warm(n):
            bank = psum.tile([P, 512], F32, name="xt")
            for i in range(n):
                nc.tensor.matmul(bank[:], lhsT=zeros[:, 0:P], rhs=zeros[:], start=True, stop=True)

        def spread_scales():
            for h in range(2):
                bank = psum.tile([P, 4, P], F32, name="xt")
                for m in range(4):
                    c = 4 * h + m
                    nc.tensor.transpose(bank[:, m, :], sv[:, c : c + 1].to_broadcast([P, P]), ident[:])
                dst = scale_row[:, 0, :].rearrange("p (n h m) -> p h n m", h=2, m=4)[:, h]
                src = bank[:].rearrange("p m n -> p n m")
                if h == 0:
                    nc.scalar.copy(out=dst, in_=src)
                else:
                    nc.vector.tensor_copy(out=dst, in_=src)
            nc.scalar.copy(out=scale_row[:, 1, :], in_=scale_row[:, 0, :])

        turns = keep.tile([P, 2, npos, PAIRS], F32, align_bytes=64)
        whole = keep.tile([P, 2, npos, PAIRS], I32, align_bytes=64)
        frac = keep.tile([P, 2, npos, PAIRS], F32, align_bytes=64)
        over = keep.tile([P, 2, npos, PAIRS], F32, align_bytes=64)
        cos_t = keep.tile([P, HALVES, TOK, ROPE], F32, align_bytes=64)
        sin_t = keep.tile([P, HALVES, TOK, ROPE], F32, align_bytes=64)

        def tables():
            for i in range(PAIRS):
                per_pos = 10000.0 ** (-2.0 * i / ROPE) / TWO_PI
                nc.vector.tensor_scalar(turns[:, 0, :, i], pos[:], per_pos, None, op0=ALU.mult)
            nc.vector.tensor_scalar(turns[:, 1], turns[:, 0], 0.25, None, op0=ALU.add)
            nc.vector.tensor_copy(out=whole[:], in_=turns[:])
            nc.vector.tensor_tensor(out=frac[:], in0=turns[:], in1=whole[:], op=ALU.subtract)
            nc.vector.scalar_tensor_tensor(
                out=over[:], in0=frac[:], scalar=0.5, in1=frac[:], op0=ALU.is_gt, op1=ALU.subtract
            )
            c = cos_t[:].rearrange("p f j (i e) -> p (f j) i e", e=2)
            s = sin_t[:].rearrange("p f j (i e) -> p (f j) i e", e=2)
            for e in range(2):
                nc.scalar.activation(c[:, :, :, e], over[:, 1], ACT.Sin, scale=-TWO_PI)
                nc.scalar.activation(s[:, :, :, e], over[:, 0], ACT.Sin, scale=(TWO_PI, -TWO_PI)[e])

        wqa = keep.tile([P, G1, 2 * QR], U8, align_bytes=64)
        wqa_s = keep.tile([P, G1, QR], U8, align_bytes=64)

        def permute_words():
            for g in range(G1):
                nc.vector.tensor_copy(
                    out=wqa[:, g].rearrange("p (j m b) -> p j m b", j=4, b=2),
                    in_=wqa_raw[:, g].rearrange("p (m j b) -> p j m b", j=4, b=2),
                )

        def permute_scales():
            for g in range(G1):
                nc.vector.tensor_copy(
                    out=wqa_s[:, g].rearrange("p (j m) -> p j m", j=4),
                    in_=wqa_raw_s[:, g].rearrange("p (m j) -> p j m", j=4),
                )

        xbf, xg, xq, xs = {}, {}, {}, {}
        cqb, cg, cq, cs = {}, {}, {}, {}
        nopes, ropes, ots = {}, {}, {}
        xts = {}

        def widen(s):
            t = work.tile([P, 2, E], BF16, align_bytes=64, name="xbf")
            xbf[s] = t
            j0 = 2 * (s % 2)
            n = 1 if s == 0 else 2
            for i in range(0, 2, n):
                nc.vector.tensor_tensor(
                    out=t[:, i : i + n, :].rearrange("p j k -> p (j k)"),
                    in0=x_tiles[s // 2][:, j0 + i : j0 + i + n, :].rearrange("p j k -> p (j k)").bitcast(FP8),
                    in1=scale_row[:, 0:n, :].rearrange("p j k -> p (j k)"),
                    op=ALU.mult,
                )

        def turn(s):
            words = xbf[s][:].rearrange("p j k -> p (j k)").bitcast(F32)
            for i in range(2):
                xt = psum.tile([P, G1, 2, P], F32, name="xt")
                xts[s, i] = xt
                for g in range(G1):
                    for u in range(2):
                        lo = 512 * i + 256 * g
                        nc.tensor.transpose(xt[:, g, u, :], words[:, lo + u : lo + 256 : 2], ident[:])

        def take_x(s):
            t = work.tile([P, 2, G1, P, 4], BF16, align_bytes=64, name="xg")
            xg[s] = t
            for i in range(2):
                nc.scalar.copy(
                    out=t[:, i].rearrange("p g r t -> p (g r t)").bitcast(F32),
                    in_=xts[s, i][:].rearrange("p g u r -> p g r u"),
                )

        def quant_x(s):
            q = work.tile([P, 2, G1, P], U32, align_bytes=64, name="xq")
            sc = work.tile([P, 2, G1, P], U8, align_bytes=64, name="xs")
            xq[s], xs[s] = q, sc
            nc.vector.quantize_mx(
                out=q[:].rearrange("p i g r -> p (i g r)").bitcast(FP8X4),
                scales=sc[:].rearrange("p i g r -> p (i g r)"),
                in_=xg[s][:].rearrange("p i g r t -> p (i g r t)"),
            )

        def first(s):
            for i in range(2):
                acc = psum.tile([P, 4, P], F32, name="cqp")
                cqb[s, i] = acc
                for j in range(4):
                    for g in range(G1):
                        nc.tensor.matmul_mx(
                            out=acc[:, j, :],
                            lhsT=wqa[:, g, 2 * P * j : 2 * P * (j + 1)].bitcast(FP4X4),
                            lhsT_scale=wqa_s[:, g, P * j : P * (j + 1)],
                            rhs=xq[s][:, i, g, :].bitcast(FP8X4),
                            rhs_scale=xs[s][:, i, g, :],
                            start=(g == 0),
                            stop=(g == G1 - 1),
                        )

        def take_cq(s):
            t = work.tile([P, 2, P, 4], BF16, align_bytes=64, name="cg")
            cg[s] = t
            for i in range(2):
                nc.scalar.copy(out=t[:, i], in_=cqb[s, i][:].rearrange("p j r -> p r j"))

        def quant_cq(s):
            q = work.tile([P, 2, P], U32, align_bytes=64, name="cq")
            sc = work.tile([P, 2, P], U8, align_bytes=64, name="cs")
            cq[s], cs[s] = q, sc
            nc.vector.quantize_mx(
                out=q[:].rearrange("p i r -> p (i r)").bitcast(FP8X4),
                scales=sc[:].rearrange("p i r -> p (i r)"),
                in_=cg[s][:].rearrange("p i r t -> p (i r t)"),
            )

        def second(s):
            if s % 2 == 0:
                rp = psum_r.tile([P, TOK, H * ROPE], F32, name="rope")
                ropes[s // 2] = rp
            npe = psum_n.tile([P, 2, nb], F32, name="nope")
            nopes[s] = npe
            rp = ropes[s // 2]
            for i in range(2):
                for dst, lo, hi in ((npe[:, i, :], 0, nb), (rp[:, 2 * (s % 2) + i, :], nb, H * QH)):
                    nc.tensor.matmul_mx(
                        out=dst,
                        lhsT=cq[s][:, i, :].bitcast(FP8X4),
                        lhsT_scale=cs[s][:, i, :],
                        rhs=wqb[:, 2 * lo : 2 * hi].bitcast(FP4X4),
                        rhs_scale=wqb_s[:, lo:hi],
                        start=True,
                        stop=True,
                    )

        def take_nope(s):
            if s % 2 == 0:
                o = outp.tile([P, H, TOK, QH], F32, align_bytes=64, name="o")
                ots[s // 2] = o
            j0 = 2 * (s % 2)
            nc.scalar.copy(
                out=ots[s // 2][:, :, j0 : j0 + 2, 0:NOPE].rearrange("p h j c -> p j h c"),
                in_=nopes[s][:].rearrange("p j (h c) -> p j h c", h=H),
            )

        ras, rbs = {}, {}

        def views(grp, j0, j1):
            src = ropes[grp][:, j0:j1, :].rearrange("p j (h i e) -> p j h i e", h=H, e=2)
            shape = [P, j1 - j0, H, ROPE]
            cosv = cos_t[:, grp % HALVES, j0:j1, :].unsqueeze(2).to_broadcast(shape)
            sinv = sin_t[:, grp % HALVES, j0:j1, :].unsqueeze(2).to_broadcast(shape)
            return src, cosv, sinv

        def rope_cos(grp, j0, j1):
            if j0 == 0:
                ra = work.tile([P, TOK, H, ROPE], F32, align_bytes=64, name="ra")
                rb = work.tile([P, TOK, H, ROPE], F32, align_bytes=64, name="rb")
                ras[grp], rbs[grp] = ra, rb
            src, cosv, sinv = views(grp, j0, j1)
            nc.vector.tensor_tensor(
                out=ras[grp][:, j0:j1], in0=src.rearrange("p j h i e -> p j h (i e)"), in1=cosv, op=ALU.mult
            )

        def rope_sin(grp, j0, j1):
            src, cosv, sinv = views(grp, j0, j1)
            nc.vector.tensor_tensor(
                out=rbs[grp][:, j0:j1].rearrange("p j h (i e) -> p j h i e", e=2),
                in0=src[:, :, :, :, ::-1],
                in1=sinv.rearrange("p j h (i e) -> p j h i e", e=2),
                op=ALU.mult,
            )

        def rope_add(eng, grp, j0, j1):
            eng.tensor_tensor(
                out=ots[grp][:, :, j0:j1, NOPE:].rearrange("p h j c -> p j h c"),
                in0=ras[grp][:, j0:j1],
                in1=rbs[grp][:, j0:j1],
                op=ALU.add,
            )

        def store(grp, j0, nj):
            dst = out[grp // HALVES].rearrange("h (f p j) c -> f p h j c", f=HALVES, j=TOK)[grp % HALVES]
            nc.sync.dma_start(out=dst[:, :, j0 : j0 + nj, :], in_=ots[grp][:, :, j0 : j0 + nj, :])

        warm(5)
        tables()
        permute_words()
        spread_scales()
        warm(3)
        widen(0)
        permute_scales()
        for s in range(STEPS + 8):
            if 0 <= s - 2 < STEPS:
                quant_x(s - 2)
            if s + 1 < STEPS:
                widen(s + 1)
            if 0 <= s - 4 < STEPS:
                quant_cq(s - 4)
            k = s - 7
            if 0 <= k < STEPS:
                grp = k // 2
                last = grp == GROUPS - 1
                if grp > 0 and k % 2 == (0 if last else 1):
                    rope_sin(grp - 1, TOK - 1, TOK)
                    rope_add(nc.gpsimd, grp - 1, 0, TOK)
                    store(grp - 1, 0, TOK)
                if last:
                    j0 = 2 * (k % 2)
                    rope_cos(grp, j0, j0 + 2)
                    rope_sin(grp, j0, j0 + 2)
                    rope_add(nc.vector, grp, j0, j0 + 2)
                    store(grp, j0, 2)
                elif k % 2 == 1:
                    rope_cos(grp, 0, TOK)
                    rope_sin(grp, 0, TOK - 1)
            if 0 <= s - 3 < STEPS:
                first(s - 3)
                take_cq(s - 3)
            if s < STEPS:
                turn(s)
                take_x(s)
            if 0 <= s - 5 < STEPS:
                second(s - 5)
                take_nope(s - 5)
